import numpy as np
import ml_dtypes


def mxq(x, axis, fmt="e4m3"):
    dtype, down = {"e4m3": (ml_dtypes.float8_e4m3fn, 7), "e5m2": (ml_dtypes.float8_e5m2, 14)}[fmt]
    v = np.moveaxis(np.asarray(x, np.float32).astype(ml_dtypes.bfloat16).astype(np.float64), axis, -1)
    blocks = v.reshape(v.shape[:-1] + (-1, 32))
    amax = np.abs(blocks).max(-1, keepdims=True)
    byte = np.maximum(np.where(amax > 0, np.frexp(amax)[1] - 1 + 127, 0) - down, 1)
    scale = np.exp2(byte - 127.0)
    codes = (blocks / scale).astype(np.float32).astype(dtype).astype(np.float64)
    return np.moveaxis((codes * scale).reshape(v.shape), -1, axis)


WIDE = False


def mx_kscale(k):
    if not WIDE:
        return np.ones(k)
    levels = np.array([30, -30])
    if k % 512:
        return np.exp2(np.random.permutation(np.resize(levels, k // 32))).repeat(32)
    a = np.empty((k // 512, 16))
    for p in range(k // 512):
        a[p, :8] = np.random.permutation(np.resize(levels, 8))
        for g in range(8):
            far = levels[np.abs(levels - a[p, g]) >= 10]
            a[p, g + 8] = far[np.random.randint(len(far))]
    return np.exp2(a.ravel()).repeat(32)


BF16 = ml_dtypes.bfloat16


def bf(x):
    return np.asarray(x, np.float32).astype(BF16)


def f64(x):
    return np.asarray(x).astype(np.float64)


E2M1 = np.array([0.0, 0.5, 1.0, 1.5, 2.0, 3.0, 4.0, 6.0, -0.0, -0.5, -1.0, -1.5, -2.0, -3.0, -4.0, -6.0])


def pack_weight(w, fmt):
    k, n = w.shape
    w = f64(bf(w)).reshape(k // 32, 32, n)
    amax = np.abs(w).max(1)
    if fmt == "e4m3":
        byte = np.frexp(amax)[1] - 1 + 127 - 7
    else:
        mant, ex = np.frexp(amax / 6.0)
        byte = np.where(mant > 0.5, ex, ex - 1) + 127
    byte = np.clip(np.where(amax > 0, byte, 1), 1, 254)
    scaled = (w * np.exp2(127.0 - byte)[:, None, :]).reshape(k, n).astype(np.float32)
    by_word = np.ascontiguousarray(scaled.reshape(k // 512, 128, 4, n).transpose(0, 1, 3, 2))
    if fmt == "e4m3":
        words = by_word.astype(ml_dtypes.float8_e4m3fn).view(np.uint8)
    else:
        c = by_word.astype(ml_dtypes.float4_e2m1fn).view(np.uint8) & 0xF
        words = c[..., 0::2] | (c[..., 1::2] << 4)
    return np.ascontiguousarray(words), np.ascontiguousarray(byte.astype(np.uint8).reshape(k // 512, 16, n))


def unpack_weight(words, scales, fmt):
    g, p, n, _ = words.shape
    if fmt == "e4m3":
        vals = np.ascontiguousarray(words).view(ml_dtypes.float8_e4m3fn).astype(np.float64)
    else:
        nib = np.empty((g, p, n, 4), np.uint8)
        nib[..., 0::2] = words & 0xF
        nib[..., 1::2] = words >> 4
        vals = E2M1[nib]
    vals = vals * np.repeat(np.exp2(scales.astype(np.float64) - 127.0), 8, axis=1)[..., None]
    return vals.transpose(0, 1, 3, 2).reshape(g * 512, n)

def pack4(w):
    words, scales = pack_weight(w, "e2m1")
    return words.reshape(words.shape[0], 128, -1), scales


def unpack4(words, scales):
    return unpack_weight(words.reshape(words.shape[0], 128, -1, 2), scales, "e2m1")


B, T, E, H, KV, BLK = 1, 512, 2048, 16, 1, 32
HD = E // H
ROPE_BASE = 10000.0


def rotate_half(t):
    d = t.shape[-1] // 2
    return np.concatenate([-t[..., d:], t[..., :d]], axis=-1)


def rope_tables():
    pos = ROPE_BASE ** ((-2.0 * np.arange(0, HD, 2) - 1.0) / HD)
    angles = np.arange(T)[:, None] * pos[None, :]
    rot = np.concatenate([angles, angles], axis=-1)
    return np.cos(rot), np.sin(rot)


def setup_inputs():
    s = mx_kscale(E)
    x = bf(np.random.standard_normal((B, T, E)) * s)
    words, scales = pack4(np.random.standard_normal((E, (H + 2 * KV) * HD)) * 1.25 * E ** -0.5 / s[:, None])
    return {"x": x, "w_attn_words": words, "w_attn_scales": scales}


def reference(x, w_attn_words, w_attn_scales):
    qkv = mxq(f64(x), 2, "e5m2") @ unpack4(w_attn_words, w_attn_scales)
    q = qkv[..., : H * HD].reshape(B, T, H, HD).transpose(0, 2, 1, 3)
    k = qkv[..., H * HD : (H + KV) * HD].reshape(B, T, KV, HD).transpose(0, 2, 1, 3)
    v = qkv[..., (H + KV) * HD :].reshape(B, T, KV, HD).transpose(0, 2, 1, 3)
    cos, sin = rope_tables()
    q = q * cos + rotate_half(q) * sin
    k = k * cos + rotate_half(k) * sin
    return q, k, v

@@ -1,0 +1,264 @@
+import math
+from contextlib import ExitStack
+
+import concourse.mybir as mybir
+from concourse.masks import make_identity
+
+T, E, H, HD = 512, 2048, 16, 128
+COLS = (H + 2) * HD
+ROPE_BASE = 10000.0
+FLOPS = 2 * T * E * COLS
+
+F32 = mybir.dt.float32
+BF16 = mybir.dt.bfloat16
+I32 = mybir.dt.int32
+U32 = mybir.dt.uint32
+U8 = mybir.dt.uint8
+E5M2X4 = mybir.dt.float8_e5m2_x4
+E2M1X4 = mybir.dt.float4_e2m1fn_x4
+ALU = mybir.AluOpType
+SIN = mybir.ActivationFunctionType.Sin
+
+P = 128
+TILES = T // P
+PASSES = E // 512
+HALF = HD // 2
+BANK = 512
+BANKS = 8
+CHUNKS = [(c0, min(BANK, COLS - c0)) for c0 in range(0, COLS, BANK)]
+KV = len(CHUNKS) - 1
+SCALE_RUNS = [[0], [1, 2, 3, 4]]
+
+
+def tile_multiqueryattention_pa_kernel(tc, x, w_words, w_scales, out_q, out_k, out_v):
+    nc = tc.nc
+    x_rows = x[0].rearrange("(p j) k -> p j k", j=TILES)
+    w_rows = w_words.rearrange("g p b -> p g b")
+    q_rows = out_q[0].rearrange("h (p j) d -> p h j d", j=TILES)
+    k_rows = out_k[0, 0].rearrange("(p j) d -> p j d", j=TILES)
+    v_rows = out_v[0, 0].rearrange("(p j) d -> p j d", j=TILES)
+
+    with ExitStack() as ctx:
+        keep = ctx.enter_context(tc.tile_pool(name="keep", bufs=1))
+        work = ctx.enter_context(tc.tile_pool(name="work", bufs=4))
+        psum = ctx.enter_context(tc.psum_pool(name="psum", bufs=1))
+        ctx.enter_context(tc.manual_schedule())
+
+        banks_taken = []
+
+        def take_bank():
+            b = len(banks_taken) % BANKS
+            bank = psum.tile([P, BANK], F32, name="bank%d" % b, tag="bank%d" % b)
+            banks_taken.append(b)
+            return bank
+
+        x_half = {}
+        w_pass = {}
+        w_plane = {}
+
+        def load_x(j, pieces):
+            width = E // pieces
+            for i in range(pieces):
+                xt = keep.tile([P, width], BF16, name="x%d_%d" % (j, i), align_bytes=64)
+                nc.sync.dma_start(out=xt[:], in_=x_rows[:, j, i * width : (i + 1) * width])
+                for s in range(2 // pieces):
+                    x_half[(j, i + s)] = xt[:, s * (E // 2) : (s + 1) * (E // 2)]
+
+        def load_w(c, pieces):
+            c0, n = CHUNKS[c]
+            count = PASSES // pieces
+            for i in range(pieces):
+                wt = keep.tile([P, count, 2 * n], U8, name="w%d_%d" % (c, i), align_bytes=64)
+                nc.sync.dma_start(
+                    out=wt[:].bitcast(I32),
+                    in_=w_rows[:, i * count : (i + 1) * count, 2 * c0 : 2 * (c0 + n)].bitcast(I32),
+                )
+                for g in range(count):
+                    w_pass[(c, i * count + g)] = wt[:, g, :]
+
+        def load_scales(run):
+            c0 = CHUNKS[run[0]][0]
+            n = sum(CHUNKS[c][1] for c in run)
+            plane = keep.tile([P, PASSES, n], U8, name="plane%d" % run[0], align_bytes=64)
+            for r in range(4):
+                nc.sync.dma_start(
+                    out=plane[r:P:32, :, :].bitcast(I32),
+                    in_=w_scales[:, r:16:4, c0 : c0 + n].rearrange("g q n -> q g n").bitcast(I32),
+                )
+            for c in run:
+                w_plane[c] = (plane, CHUNKS[c][0] - c0)
+
+        load_x(0, 2)
+        load_x(1, 1)
+        load_scales(SCALE_RUNS[0])
+        load_w(0, 2)
+        load_x(2, 1)
+        load_x(3, 1)
+        load_scales(SCALE_RUNS[1])
+        for c in range(1, len(CHUNKS)):
+            load_w(c, 1)
+
+        token = keep.tile([P, TILES], F32)
+        nc.gpsimd.iota(token[:], [[1, TILES]], base=0, channel_multiplier=TILES, allow_small_or_imprecise_dtypes=True)
+        ident = keep.tile([P, P], F32)
+        make_identity(nc, ident[:])
+
+        fine = keep.tile([P, 8, TILES], F32)
+        for m in range(8):
+            freq = ROPE_BASE ** (-(4 * m + 1) / HD) / (2 * math.pi)
+            nc.vector.tensor_scalar(out=fine[:, m, :], in0=token[:], scalar1=freq, scalar2=None, op0=ALU.mult)
+        turns = keep.tile([P, 2, TILES, HALF], F32)
+        for n in range(8):
+            nc.vector.tensor_scalar(
+                out=turns[:, 0, :, 8 * n : 8 * (n + 1)],
+                in0=fine[:].rearrange("p m j -> p j m"),
+                scalar1=ROPE_BASE ** (-32 * n / HD),
+                scalar2=None,
+                op0=ALU.mult,
+            )
+        nc.vector.tensor_scalar(out=turns[:, 1, :, :], in0=turns[:, 0, :, :], scalar1=0.25, scalar2=None, op0=ALU.add)
+        whole = keep.tile([P, 2, TILES, HALF], I32)
+        nc.vector.tensor_copy(out=whole[:], in_=turns[:])
+        frac = keep.tile([P, 2, TILES, HALF], F32)
+        nc.vector.tensor_tensor(out=frac[:], in0=turns[:], in1=whole[:], op=ALU.subtract)
+
+        table = [keep.tile([P, 2, 2, HD], F32, name="table%d" % ph) for ph in range(2)]
+
+        def fill_cos(ph):
+            nc.scalar.activation(
+                out=table[ph][:, :, 0, :].rearrange("p j (o i) -> p j o i", o=2),
+                in_=frac[:, 1, 2 * ph : 2 * ph + 2, :].rearrange("p j (o i) -> p j o i", o=1).to_broadcast([P, 2, 2, HALF]),
+                func=SIN,
+                scale=2 * math.pi,
+            )
+
+        def fill_sin(ph):
+            for o, sign in ((0, 1.0), (1, -1.0)):
+                nc.scalar.activation(
+                    out=table[ph][:, :, 1, o * HALF : (o + 1) * HALF],
+                    in_=frac[:, 0, 2 * ph : 2 * ph + 2, :],
+                    func=SIN,
+                    scale=sign * 2 * math.pi,
+                )
+
+        grouped = {}
+        x_codes = {}
+        x_plane = {}
+
+        def transpose_half(j, s):
+            words = x_half[(j, s)].bitcast(F32)
+            bank = take_bank()
+            for g in range(2):
+                for u in range(2):
+                    col = (2 * g + u) * P
+                    nc.tensor.transpose(bank[:, col : col + P], words[:, 256 * g + u : 256 * (g + 1) : 2], ident[:])
+            gt = work.tile([P, E // 2], BF16, name="grouped", align_bytes=64)
+            nc.scalar.copy(
+                out=gt[:].bitcast(F32).rearrange("p (g r u) -> p g r u", g=2, u=2),
+                in_=bank[:].rearrange("p (g u r) -> p g r u", g=2, u=2),
+            )
+            grouped[(j, s)] = gt
+
+        def quantize_half(j, s):
+            codes = keep.tile([P, 2 * P], U32, name="codes%d_%d" % (j, s), align_bytes=64)
+            plane = keep.tile([P, 2 * P], U8, name="xplane%d_%d" % (j, s), align_bytes=64)
+            nc.vector.quantize_mx(out=codes[:].bitcast(E5M2X4), scales=plane[:], in_=grouped[(j, s)][:])
+            x_codes[(j, s)] = codes
+            x_plane[(j, s)] = plane
+
+        def project(j, c):
+            n = CHUNKS[c][1]
+            plane, off = w_plane[c]
+            bank = take_bank()
+            for g in range(PASSES):
+                cols = slice((g % 2) * P, (g % 2 + 1) * P)
+                nc.tensor.matmul_mx(
+                    out=bank[:, 0:n],
+                    lhsT=x_codes[(j, g // 2)][:, cols].bitcast(E5M2X4),
+                    lhsT_scale=x_plane[(j, g // 2)][:, cols],
+                    rhs=w_pass[(c, g)].bitcast(E2M1X4),
+                    rhs_scale=plane[:, g, off : off + n],
+                    start=(g == 0),
+                    stop=(g == PASSES - 1),
+                )
+            return bank
+
+        def multiply(j, src, prod):
+            shape = list(prod.shape)
+            nc.vector.tensor_tensor(
+                out=prod,
+                in0=src.rearrange("p (o h d) -> p o h d", o=1, d=HD).to_broadcast(shape),
+                in1=table[j // 2][:, j % 2, :, :].rearrange("p c (o d) -> p c o d", o=1).to_broadcast(shape),
+                op=ALU.mult,
+            )
+
+        def combine(engine, prod, dst):
+            engine.tensor_tensor(
+                out=dst.rearrange("p h (o i) -> p h o i", o=2),
+                in0=prod[:, 0, :, :].rearrange("p h (o i) -> p h o i", o=2),
+                in1=prod[:, 1, :, :].rearrange("p h (o i) -> p h o i", o=2)[:, :, ::-1, :],
+                op=ALU.add,
+            )
+
+        def multiply_pair(c, pair):
+            prod = work.tile([P, 2, 4, 2, HD], F32, name="prod")
+            for jj in range(2):
+                j = 2 * pair + jj
+                multiply(j, project(j, c)[:], prod[:, :, :, jj, :])
+            return prod
+
+        def store_q(c, j0, j1, src):
+            nc.sync.dma_start(out=q_rows[:, 4 * c : 4 * c + 4, j0:j1, :], in_=src)
+
+        def gpsimd_pair(c, pair):
+            prod = multiply_pair(c, pair)
+            res = keep.tile([P, 4, 2, HD], F32, name="res%d_%d" % (c, pair))
+            combine(nc.gpsimd, prod[:].rearrange("p c h j d -> p c (h j) d"), res[:].rearrange("p h j d -> p (h j) d"))
+            store_q(c, 2 * pair, 2 * pair + 2, res[:])
+
+        fill_cos(0)
+        transpose_half(0, 0)
+        transpose_half(0, 1)
+        quantize_half(0, 0)
+        fill_sin(0)
+        transpose_half(1, 0)
+        quantize_half(0, 1)
+        transpose_half(1, 1)
+        quantize_half(1, 0)
+        quantize_half(1, 1)
+        fill_cos(1)
+        fill_sin(1)
+
+        first = multiply_pair(0, 0)
+        first_res = keep.tile([P, 4, 2, HD], F32)
+        for j in (2, 3):
+            for s in range(2):
+                transpose_half(j, s)
+        for jj in range(2):
+            combine(nc.vector, first[:, :, :, jj, :], first_res[:, :, jj, :])
+            for s in range(2):
+                quantize_half(2 + jj, s)
+        store_q(0, 0, 2, first_res[:])
+
+        gpsimd_pair(0, 1)
+        for c in range(1, KV):
+            gpsimd_pair(c, 0)
+            if c < KV - 1:
+                gpsimd_pair(c, 1)
+
+        last = multiply_pair(KV - 1, 1)
+        last_res = keep.tile([P, 4, 2, HD], F32)
+        k_prod = keep.tile([P, 2, TILES, HD], F32)
+        k_res = keep.tile([P, TILES, HD], F32)
+        v_res = keep.tile([P, TILES, HD], F32)
+        for j in range(TILES):
+            bank = project(j, KV)
+            multiply(j, bank[:, 0:HD], k_prod[:, :, j : j + 1, :])
+            nc.scalar.copy(out=v_res[:, j, :], in_=bank[:, HD : 2 * HD])
+            if j % 2 == 0:
+                jj = j // 2
+                combine(nc.vector, last[:, :, :, jj, :], last_res[:, :, jj, :])
+                store_q(KV - 1, 2 + jj, 3 + jj, last_res[:, :, jj : jj + 1, :])
+        nc.scalar.dma_start(out=v_rows, in_=v_res[:])
+        combine(nc.vector, k_prod[:], k_res[:])
+        nc.sync.dma_start(out=k_rows, in_=k_res[:])

@@ -27,7 +27,7 @@ BANK = 512
 BANKS = 8
 CHUNKS = [(c0, min(BANK, COLS - c0)) for c0 in range(0, COLS, BANK)]
 KV = len(CHUNKS) - 1
-SCALE_RUNS = [[0], [1, 2, 3, 4]]
+SCALE_RUNS = [[0], [1], [2, 3, 4]]
 
 
 def tile_multiqueryattention_pa_kernel(tc, x, w_words, w_scales, out_q, out_k, out_v):
@@ -89,13 +89,15 @@ def tile_multiqueryattention_pa_kernel(tc, x, w_words, w_scales, out_q, out_k, o
                 w_plane[c] = (plane, CHUNKS[c][0] - c0)
 
         load_x(0, 2)
-        load_x(1, 1)
+        load_x(1, 2)
         load_scales(SCALE_RUNS[0])
         load_w(0, 2)
         load_x(2, 1)
         load_x(3, 1)
         load_scales(SCALE_RUNS[1])
-        for c in range(1, len(CHUNKS)):
+        load_w(1, 1)
+        load_scales(SCALE_RUNS[2])
+        for c in range(2, len(CHUNKS)):
             load_w(c, 1)
 
         token = keep.tile([P, TILES], F32)
@@ -255,10 +257,9 @@ def tile_multiqueryattention_pa_kernel(tc, x, w_words, w_scales, out_q, out_k, o
             bank = project(j, KV)
             multiply(j, bank[:, 0:HD], k_prod[:, :, j : j + 1, :])
             nc.scalar.copy(out=v_res[:, j, :], in_=bank[:, HD : 2 * HD])
-            if j % 2 == 0:
-                jj = j // 2
-                combine(nc.vector, last[:, :, :, jj, :], last_res[:, :, jj, :])
-                store_q(KV - 1, 2 + jj, 3 + jj, last_res[:, :, jj : jj + 1, :])
         nc.scalar.dma_start(out=v_rows, in_=v_res[:])
+        for jj in range(2):
+            combine(nc.vector, last[:, :, :, jj, :], last_res[:, :, jj, :])
+            store_q(KV - 1, 2 + jj, 3 + jj, last_res[:, :, jj : jj + 1, :])
         combine(nc.vector, k_prod[:], k_res[:])
         nc.sync.dma_start(out=k_rows, in_=k_res[:])

@@ -40,7 +40,7 @@ def tile_multiqueryattention_pa_kernel(tc, x, w_words, w_scales, out_q, out_k, o
 
     with ExitStack() as ctx:
         keep = ctx.enter_context(tc.tile_pool(name="keep", bufs=1))
-        work = ctx.enter_context(tc.tile_pool(name="work", bufs=4))
+        work = ctx.enter_context(tc.tile_pool(name="work", bufs=5))
         psum = ctx.enter_context(tc.psum_pool(name="psum", bufs=1))
         ctx.enter_context(tc.manual_schedule())
 
@@ -168,8 +168,8 @@ def tile_multiqueryattention_pa_kernel(tc, x, w_words, w_scales, out_q, out_k, o
             x_codes[(j, s)] = codes
             x_plane[(j, s)] = plane
 
-        def project(j, c):
-            n = CHUNKS[c][1]
+        def project(j, head, heads):
+            c, lo, n = head // 4, (head % 4) * HD, heads * HD
             plane, off = w_plane[c]
             bank = take_bank()
             for g in range(PASSES):
@@ -178,12 +178,12 @@ def tile_multiqueryattention_pa_kernel(tc, x, w_words, w_scales, out_q, out_k, o
                     out=bank[:, 0:n],
                     lhsT=x_codes[(j, g // 2)][:, cols].bitcast(E5M2X4),
                     lhsT_scale=x_plane[(j, g // 2)][:, cols],
-                    rhs=w_pass[(c, g)].bitcast(E2M1X4),
-                    rhs_scale=plane[:, g, off : off + n],
+                    rhs=w_pass[(c, g)][:, 2 * lo : 2 * (lo + n)].bitcast(E2M1X4),
+                    rhs_scale=plane[:, g, off + lo : off + lo + n],
                     start=(g == 0),
                     stop=(g == PASSES - 1),
                 )
-            return bank
+            return bank[:, 0:n]
 
         def multiply(j, src, prod):
             shape = list(prod.shape)
@@ -202,21 +202,17 @@ def tile_multiqueryattention_pa_kernel(tc, x, w_words, w_scales, out_q, out_k, o
                 op=ALU.add,
             )
 
-        def multiply_pair(c, pair):
-            prod = work.tile([P, 2, 4, 2, HD], F32, name="prod")
+        def multiply_pair(head, heads, pair):
+            prod = work.tile([P, 2, heads, 2, HD], F32, name="prod")
             for jj in range(2):
                 j = 2 * pair + jj
-                multiply(j, project(j, c)[:], prod[:, :, :, jj, :])
+                multiply(j, project(j, head, heads), prod[:, :, :, jj, :])
             return prod
 
-        def store_q(c, j0, j1, src):
-            nc.sync.dma_start(out=q_rows[:, 4 * c : 4 * c + 4, j0:j1, :], in_=src)
-
-        def gpsimd_pair(c, pair):
-            prod = multiply_pair(c, pair)
-            res = keep.tile([P, 4, 2, HD], F32, name="res%d_%d" % (c, pair))
-            combine(nc.gpsimd, prod[:].rearrange("p c h j d -> p c (h j) d"), res[:].rearrange("p h j d -> p (h j) d"))
-            store_q(c, 2 * pair, 2 * pair + 2, res[:])
+        def finish_pair(engine, prod, head, heads, pair):
+            res = keep.tile([P, heads, 2, HD], F32, name="res%d_%d" % (head, pair))
+            combine(engine, prod[:].rearrange("p c h j d -> p c (h j) d"), res[:].rearrange("p h j d -> p (h j) d"))
+            nc.sync.dma_start(out=q_rows[:, head : head + heads, 2 * pair : 2 * pair + 2, :], in_=res[:])
 
         fill_cos(0)
         transpose_half(0, 0)
@@ -231,7 +227,7 @@ def tile_multiqueryattention_pa_kernel(tc, x, w_words, w_scales, out_q, out_k, o
         fill_cos(1)
         fill_sin(1)
 
-        first = multiply_pair(0, 0)
+        first = multiply_pair(0, 4, 0)
         first_res = keep.tile([P, 4, 2, HD], F32)
         for j in (2, 3):
             for s in range(2):
@@ -240,26 +236,23 @@ def tile_multiqueryattention_pa_kernel(tc, x, w_words, w_scales, out_q, out_k, o
             combine(nc.vector, first[:, :, :, jj, :], first_res[:, :, jj, :])
             for s in range(2):
                 quantize_half(2 + jj, s)
-        store_q(0, 0, 2, first_res[:])
+        nc.sync.dma_start(out=q_rows[:, 0:4, 0:2, :], in_=first_res[:])
 
-        gpsimd_pair(0, 1)
-        for c in range(1, KV):
-            gpsimd_pair(c, 0)
-            if c < KV - 1:
-                gpsimd_pair(c, 1)
+        for head, heads, pair in [(0, 4, 1), (4, 4, 0), (4, 4, 1), (8, 4, 0), (8, 4, 1), (12, 2, 0)]:
+            finish_pair(nc.gpsimd, multiply_pair(head, heads, pair), head, heads, pair)
 
-        last = multiply_pair(KV - 1, 1)
-        last_res = keep.tile([P, 4, 2, HD], F32)
+        late = [(head, pair, multiply_pair(head, 2, pair)) for head, pair in [(12, 1), (14, 0), (14, 1)]]
         k_prod = keep.tile([P, 2, TILES, HD], F32)
         k_res = keep.tile([P, TILES, HD], F32)
         v_res = keep.tile([P, TILES, HD], F32)
         for j in range(TILES):
-            bank = project(j, KV)
+            bank = project(j, H, 2)
             multiply(j, bank[:, 0:HD], k_prod[:, :, j : j + 1, :])
             nc.scalar.copy(out=v_res[:, j, :], in_=bank[:, HD : 2 * HD])
-        nc.scalar.dma_start(out=v_rows, in_=v_res[:])
-        for jj in range(2):
-            combine(nc.vector, last[:, :, :, jj, :], last_res[:, :, jj, :])
-            store_q(KV - 1, 2 + jj, 3 + jj, last_res[:, :, jj : jj + 1, :])
+            if j % 2 == 1:
+                nc.scalar.dma_start(out=v_rows[:, j - 1 : j + 1, :], in_=v_res[:, j - 1 : j + 1, :])
+            if j >= 1:
+                head, pair, prod = late[j - 1]
+                finish_pair(nc.vector, prod, head, 2, pair)
         combine(nc.vector, k_prod[:], k_res[:])
         nc.sync.dma_start(out=k_rows, in_=k_res[:])

@@ -214,12 +214,27 @@ def tile_multiqueryattention_pa_kernel(tc, x, w_words, w_scales, out_q, out_k, o
             combine(engine, prod[:].rearrange("p c h j d -> p c (h j) d"), res[:].rearrange("p h j d -> p (h j) d"))
             nc.sync.dma_start(out=q_rows[:, head : head + heads, 2 * pair : 2 * pair + 2, :], in_=res[:])
 
+        unread = psum.tile([P, BANK], F32, name="unread", tag="bank%d" % (BANKS - 1))
+
+        def warm_up(n):
+            nc.tensor.matmul(
+                out=unread[:, 0:n],
+                lhsT=token[:, 0:1].to_broadcast([P, P]),
+                rhs=token[:, 0:1].to_broadcast([P, n]),
+                start=True,
+                stop=True,
+            )
+
+        warm_up(2 * P)
+        warm_up(2 * P)
         fill_cos(0)
         transpose_half(0, 0)
+        warm_up(P)
         transpose_half(0, 1)
         quantize_half(0, 0)
         fill_sin(0)
         transpose_half(1, 0)
+        warm_up(P)
         quantize_half(0, 1)
         transpose_half(1, 1)
         quantize_half(1, 0)

import math
from contextlib import ExitStack

import concourse.mybir as mybir
from concourse.masks import make_identity

T, E, H, HD = 512, 2048, 16, 128
COLS = (H + 2) * HD
ROPE_BASE = 10000.0
FLOPS = 2 * T * E * COLS

F32 = mybir.dt.float32
BF16 = mybir.dt.bfloat16
I32 = mybir.dt.int32
U32 = mybir.dt.uint32
U8 = mybir.dt.uint8
E5M2X4 = mybir.dt.float8_e5m2_x4
E2M1X4 = mybir.dt.float4_e2m1fn_x4
ALU = mybir.AluOpType
SIN = mybir.ActivationFunctionType.Sin

P = 128
TILES = T // P
PASSES = E // 512
HALF = HD // 2
BANK = 512
BANKS = 8
CHUNKS = [(c0, min(BANK, COLS - c0)) for c0 in range(0, COLS, BANK)]
KV = len(CHUNKS) - 1
SCALE_RUNS = [[0], [1], [2, 3, 4]]


def tile_multiqueryattention_pa_kernel(tc, x, w_words, w_scales, out_q, out_k, out_v):
    nc = tc.nc
    x_rows = x[0].rearrange("(p j) k -> p j k", j=TILES)
    w_rows = w_words.rearrange("g p b -> p g b")
    q_rows = out_q[0].rearrange("h (p j) d -> p h j d", j=TILES)
    k_rows = out_k[0, 0].rearrange("(p j) d -> p j d", j=TILES)
    v_rows = out_v[0, 0].rearrange("(p j) d -> p j d", j=TILES)

    with ExitStack() as ctx:
        keep = ctx.enter_context(tc.tile_pool(name="keep", bufs=1))
        work = ctx.enter_context(tc.tile_pool(name="work", bufs=5))
        psum = ctx.enter_context(tc.psum_pool(name="psum", bufs=1))
        ctx.enter_context(tc.manual_schedule())

        banks_taken = []

        def take_bank():
            b = len(banks_taken) % BANKS
            bank = psum.tile([P, BANK], F32, name="bank%d" % b, tag="bank%d" % b)
            banks_taken.append(b)
            return bank

        x_half = {}
        w_pass = {}
        w_plane = {}

        def load_x(j, pieces):
            width = E // pieces
            for i in range(pieces):
                xt = keep.tile([P, width], BF16, name="x%d_%d" % (j, i), align_bytes=64)
                nc.sync.dma_start(out=xt[:], in_=x_rows[:, j, i * width : (i + 1) * width])
                for s in range(2 // pieces):
                    x_half[(j, i + s)] = xt[:, s * (E // 2) : (s + 1) * (E // 2)]

        def load_w(c, pieces):
            c0, n = CHUNKS[c]
            count = PASSES // pieces
            for i in range(pieces):
                wt = keep.tile([P, count, 2 * n], U8, name="w%d_%d" % (c, i), align_bytes=64)
                nc.sync.dma_start(
                    out=wt[:].bitcast(I32),
                    in_=w_rows[:, i * count : (i + 1) * count, 2 * c0 : 2 * (c0 + n)].bitcast(I32),
                )
                for g in range(count):
                    w_pass[(c, i * count + g)] = wt[:, g, :]

        def load_scales(run):
            c0 = CHUNKS[run[0]][0]
            n = sum(CHUNKS[c][1] for c in run)
            plane = keep.tile([P, PASSES, n], U8, name="plane%d" % run[0], align_bytes=64)
            for r in range(4):
                nc.sync.dma_start(
                    out=plane[r:P:32, :, :].bitcast(I32),
                    in_=w_scales[:, r:16:4, c0 : c0 + n].rearrange("g q n -> q g n").bitcast(I32),
                )
            for c in run:
                w_plane[c] = (plane, CHUNKS[c][0] - c0)

        load_x(0, 2)
        load_x(1, 2)
        load_scales(SCALE_RUNS[0])
        load_w(0, 2)
        load_x(2, 1)
        load_x(3, 1)
        load_scales(SCALE_RUNS[1])
        load_w(1, 1)
        load_scales(SCALE_RUNS[2])
        for c in range(2, len(CHUNKS)):
            load_w(c, 1)

        token = keep.tile([P, TILES], F32)
        nc.gpsimd.iota(token[:], [[1, TILES]], base=0, channel_multiplier=TILES, allow_small_or_imprecise_dtypes=True)
        ident = keep.tile([P, P], F32)
        make_identity(nc, ident[:])

        fine = keep.tile([P, 8, TILES], F32)
        for m in range(8):
            freq = ROPE_BASE ** (-(4 * m + 1) / HD) / (2 * math.pi)
            nc.vector.tensor_scalar(out=fine[:, m, :], in0=token[:], scalar1=freq, scalar2=None, op0=ALU.mult)
        turns = keep.tile([P, 2, TILES, HALF], F32)
        for n in range(8):
            nc.vector.tensor_scalar(
                out=turns[:, 0, :, 8 * n : 8 * (n + 1)],
                in0=fine[:].rearrange("p m j -> p j m"),
                scalar1=ROPE_BASE ** (-32 * n / HD),
                scalar2=None,
                op0=ALU.mult,
            )
        nc.vector.tensor_scalar(out=turns[:, 1, :, :], in0=turns[:, 0, :, :], scalar1=0.25, scalar2=None, op0=ALU.add)
        whole = keep.tile([P, 2, TILES, HALF], I32)
        nc.vector.tensor_copy(out=whole[:], in_=turns[:])
        frac = keep.tile([P, 2, TILES, HALF], F32)
        nc.vector.tensor_tensor(out=frac[:], in0=turns[:], in1=whole[:], op=ALU.subtract)

        table = [keep.tile([P, 2, 2, HD], F32, name="table%d" % ph) for ph in range(2)]

        def fill_cos(ph):
            nc.scalar.activation(
                out=table[ph][:, :, 0, :].rearrange("p j (o i) -> p j o i", o=2),
                in_=frac[:, 1, 2 * ph : 2 * ph + 2, :].rearrange("p j (o i) -> p j o i", o=1).to_broadcast([P, 2, 2, HALF]),
                func=SIN,
                scale=2 * math.pi,
            )

        def fill_sin(ph):
            for o, sign in ((0, 1.0), (1, -1.0)):
                nc.scalar.activation(
                    out=table[ph][:, :, 1, o * HALF : (o + 1) * HALF],
                    in_=frac[:, 0, 2 * ph : 2 * ph + 2, :],
                    func=SIN,
                    scale=sign * 2 * math.pi,
                )

        grouped = {}
        x_codes = {}
        x_plane = {}

        def transpose_half(j, s):
            words = x_half[(j, s)].bitcast(F32)
            bank = take_bank()
            for g in range(2):
                for u in range(2):
                    col = (2 * g + u) * P
                    nc.tensor.transpose(bank[:, col : col + P], words[:, 256 * g + u : 256 * (g + 1) : 2], ident[:])
            gt = work.tile([P, E // 2], BF16, name="grouped", align_bytes=64)
            nc.scalar.copy(
                out=gt[:].bitcast(F32).rearrange("p (g r u) -> p g r u", g=2, u=2),
                in_=bank[:].rearrange("p (g u r) -> p g r u", g=2, u=2),
            )
            grouped[(j, s)] = gt

        def quantize_half(j, s):
            codes = keep.tile([P, 2 * P], U32, name="codes%d_%d" % (j, s), align_bytes=64)
            plane = keep.tile([P, 2 * P], U8, name="xplane%d_%d" % (j, s), align_bytes=64)
            nc.vector.quantize_mx(out=codes[:].bitcast(E5M2X4), scales=plane[:], in_=grouped[(j, s)][:])
            x_codes[(j, s)] = codes
            x_plane[(j, s)] = plane

        def project(j, head, heads):
            c, lo, n = head // 4, (head % 4) * HD, heads * HD
            plane, off = w_plane[c]
            bank = take_bank()
            for g in range(PASSES):
                cols = slice((g % 2) * P, (g % 2 + 1) * P)
                nc.tensor.matmul_mx(
                    out=bank[:, 0:n],
                    lhsT=x_codes[(j, g // 2)][:, cols].bitcast(E5M2X4),
                    lhsT_scale=x_plane[(j, g // 2)][:, cols],
                    rhs=w_pass[(c, g)][:, 2 * lo : 2 * (lo + n)].bitcast(E2M1X4),
                    rhs_scale=plane[:, g, off + lo : off + lo + n],
                    start=(g == 0),
                    stop=(g == PASSES - 1),
                )
            return bank[:, 0:n]

        def multiply(j, src, prod):
            shape = list(prod.shape)
            nc.vector.tensor_tensor(
                out=prod,
                in0=src.rearrange("p (o h d) -> p o h d", o=1, d=HD).to_broadcast(shape),
                in1=table[j // 2][:, j % 2, :, :].rearrange("p c (o d) -> p c o d", o=1).to_broadcast(shape),
                op=ALU.mult,
            )

        def combine(engine, prod, dst):
            engine.tensor_tensor(
                out=dst.rearrange("p h (o i) -> p h o i", o=2),
                in0=prod[:, 0, :, :].rearrange("p h (o i) -> p h o i", o=2),
                in1=prod[:, 1, :, :].rearrange("p h (o i) -> p h o i", o=2)[:, :, ::-1, :],
                op=ALU.add,
            )

        def multiply_pair(head, heads, pair):
            prod = work.tile([P, 2, heads, 2, HD], F32, name="prod")
            for jj in range(2):
                j = 2 * pair + jj
                multiply(j, project(j, head, heads), prod[:, :, :, jj, :])
            return prod

        def finish_pair(engine, prod, head, heads, pair):
            res = keep.tile([P, heads, 2, HD], F32, name="res%d_%d" % (head, pair))
            combine(engine, prod[:].rearrange("p c h j d -> p c (h j) d"), res[:].rearrange("p h j d -> p (h j) d"))
            nc.sync.dma_start(out=q_rows[:, head : head + heads, 2 * pair : 2 * pair + 2, :], in_=res[:])

        unread = psum.tile([P, BANK], F32, name="unread", tag="bank%d" % (BANKS - 1))

        def warm_up(n):
            nc.tensor.matmul(
                out=unread[:, 0:n],
                lhsT=token[:, 0:1].to_broadcast([P, P]),
                rhs=token[:, 0:1].to_broadcast([P, n]),
                start=True,
                stop=True,
            )

        warm_up(2 * P)
        warm_up(2 * P)
        fill_cos(0)
        transpose_half(0, 0)
        warm_up(P)
        transpose_half(0, 1)
        quantize_half(0, 0)
        fill_sin(0)
        transpose_half(1, 0)
        warm_up(P)
        quantize_half(0, 1)
        transpose_half(1, 1)
        quantize_half(1, 0)
        quantize_half(1, 1)
        fill_cos(1)
        fill_sin(1)

        first = multiply_pair(0, 4, 0)
        first_res = keep.tile([P, 4, 2, HD], F32)
        for j in (2, 3):
            for s in range(2):
                transpose_half(j, s)
        for jj in range(2):
            combine(nc.vector, first[:, :, :, jj, :], first_res[:, :, jj, :])
            for s in range(2):
                quantize_half(2 + jj, s)
        nc.sync.dma_start(out=q_rows[:, 0:4, 0:2, :], in_=first_res[:])

        for head, heads, pair in [(0, 4, 1), (4, 4, 0), (4, 4, 1), (8, 4, 0), (8, 4, 1), (12, 2, 0)]:
            finish_pair(nc.gpsimd, multiply_pair(head, heads, pair), head, heads, pair)

        late = [(head, pair, multiply_pair(head, 2, pair)) for head, pair in [(12, 1), (14, 0), (14, 1)]]
        k_prod = keep.tile([P, 2, TILES, HD], F32)
        k_res = keep.tile([P, TILES, HD], F32)
        v_res = keep.tile([P, TILES, HD], F32)
        for j in range(TILES):
            bank = project(j, H, 2)
            multiply(j, bank[:, 0:HD], k_prod[:, :, j : j + 1, :])
            nc.scalar.copy(out=v_res[:, j, :], in_=bank[:, HD : 2 * HD])
            if j % 2 == 1:
                nc.scalar.dma_start(out=v_rows[:, j - 1 : j + 1, :], in_=v_res[:, j - 1 : j + 1, :])
            if j >= 1:
                head, pair, prod = late[j - 1]
                finish_pair(nc.vector, prod, head, 2, pair)
        combine(nc.vector, k_prod[:], k_res[:])
        nc.sync.dma_start(out=k_rows, in_=k_res[:])
